import numpy as np
import ml_dtypes


def mxq(x, axis, fmt="e4m3"):
    dtype, down = {"e4m3": (ml_dtypes.float8_e4m3fn, 7), "e5m2": (ml_dtypes.float8_e5m2, 14)}[fmt]
    v = np.moveaxis(np.asarray(x, np.float32).astype(ml_dtypes.bfloat16).astype(np.float64), axis, -1)
    blocks = v.reshape(v.shape[:-1] + (-1, 32))
    amax = np.abs(blocks).max(-1, keepdims=True)
    byte = np.maximum(np.where(amax > 0, np.frexp(amax)[1] - 1 + 127, 0) - down, 1)
    scale = np.exp2(byte - 127.0)
    codes = (blocks / scale).astype(np.float32).astype(dtype).astype(np.float64)
    return np.moveaxis((codes * scale).reshape(v.shape), -1, axis)


WIDE = False


def mx_kscale(k):
    if not WIDE:
        return np.ones(k)
    levels = np.array([10, -10, 5, -5, 0])
    if k % 512:
        return np.exp2(np.random.permutation(np.resize(levels, k // 32))).repeat(32)
    a = np.empty((k // 512, 16))
    for p in range(k // 512):
        a[p, :8] = np.random.permutation(np.resize(levels, 8))
        for g in range(8):
            far = levels[np.abs(levels - a[p, g]) >= 10]
            a[p, g + 8] = far[np.random.randint(len(far))]
    return np.exp2(a.ravel()).repeat(32)


BF16 = ml_dtypes.bfloat16


def bf(x):
    return np.asarray(x, np.float32).astype(BF16)


def f64(x):
    return np.asarray(x).astype(np.float64)


B, S, H, I, R = 4, 32, 1024, 1024, 512
EPS = 1e-05


def rmsnorm(h, w):
    var = np.mean(h * h, axis=-1, keepdims=True)
    return h * (1.0 / np.sqrt(var + EPS)) * w


def silu(v):
    return v / (1.0 + np.exp(-v))


def setup_inputs():
    s, t = mx_kscale(H), mx_kscale(R)
    return {"x": bf(np.random.standard_normal((B, S, H))),
            "residual": bf(np.random.standard_normal((B, S, H))),
            "ln_w": bf((1.0 + 0.1 * np.random.standard_normal(H)) * s),
            "w_gate_v": bf(np.random.standard_normal((H, R)) / np.sqrt(H) / s[:, None] * t),
            "w_gate_u": bf(np.random.standard_normal((R, I)) / np.sqrt(R) / t[:, None]),
            "w_up_v": bf(np.random.standard_normal((H, R)) / np.sqrt(H) / s[:, None] * t),
            "w_up_u": bf(np.random.standard_normal((R, I)) / np.sqrt(R) / t[:, None])}


def reference(x, residual, ln_w, w_gate_v, w_gate_u, w_up_v, w_up_u):
    h = f64(x) + f64(residual)
    n = rmsnorm(h, f64(ln_w))
    nq = mxq(n, 2, "e4m3")
    gate_r = nq @ mxq(f64(w_gate_v), 0, "e4m3")
    up_r = nq @ mxq(f64(w_up_v), 0, "e4m3")
    gate = silu(mxq(gate_r, 2, "e4m3") @ mxq(f64(w_gate_u), 0, "e4m3"))
    up = mxq(up_r, 2, "e4m3") @ mxq(f64(w_up_u), 0, "e4m3")
    return gate * up

@@ -1,0 +1,281 @@
+import concourse.mybir as mybir
+from concourse.masks import make_identity
+
+BF16 = mybir.dt.bfloat16
+F32 = mybir.dt.float32
+U32 = mybir.dt.uint32
+U8 = mybir.dt.uint8
+FP8X4 = mybir.dt.float8_e4m3fn_x4
+ALU = mybir.AluOpType
+ACT = mybir.ActivationFunctionType
+
+P = 128
+PACK = 4
+K_PASS = P * PACK
+H = 1024
+R = 512
+I = 1024
+PASSES = H // K_PASS
+HALVES = I // 512
+EPS = 1e-05
+CHUNK = 512
+RUN = 4
+VECTOR_COLS = 256
+GATE, UP = 0, 1
+
+FLOPS = 2 * P * (2 * H * R + 2 * R * I)
+
+
+def tile_neuronllamamlp_pa_s_kernel(
+    tc, x, residual, ln_w, w_gate_v, w_gate_u, w_up_v, w_up_u, out
+):
+    nc = tc.nc
+    x_rows = x.flatten_outer_dims()
+    res_rows = residual.flatten_outer_dims()
+    out_rows = out.flatten_outer_dims()
+
+    with tc.tile_pool(name="keep", bufs=1) as keep, tc.psum_pool(
+        name="psum", bufs=1
+    ) as psum, tc.manual_schedule():
+        x_sb = keep.tile([P, PASSES, K_PASS], BF16, name="x_sb")
+        res_sb = keep.tile([P, PASSES, K_PASS], BF16, name="res_sb")
+        for g in range(PASSES):
+            cols = slice(g * K_PASS, (g + 1) * K_PASS)
+            nc.sync.dma_start(out=x_sb[:, g, :], in_=x_rows[:, cols])
+            nc.sync.dma_start(out=res_sb[:, g, :], in_=res_rows[:, cols])
+        ln_sb = keep.tile([P, PASSES, PACK], BF16, name="ln_sb")
+        nc.scalar.dma_start(out=ln_sb[:], in_=ln_w.rearrange("(g p j) -> p g j", p=P, j=PACK))
+
+        chunk_views = []
+        for w in (w_gate_v, w_up_v):
+            for g in range(PASSES):
+                rows = w[g * K_PASS : (g + 1) * K_PASS, :]
+                chunk_views.append(rows.rearrange("(p j) r -> p j r", j=PACK))
+        for w in (w_gate_u, w_up_u):
+            for half in range(HALVES):
+                cols = w[:, half * CHUNK : (half + 1) * CHUNK]
+                chunk_views.append(cols.rearrange("(p j) i -> p j i", j=PACK))
+
+        raws, groupeds, codes, scales = [], [], [], []
+        for c, view in enumerate(chunk_views):
+            raws.append(keep.tile([P, PACK, CHUNK], BF16, name="raw%d" % c))
+            groupeds.append(keep.tile([P, CHUNK, PACK], BF16, name="grouped%d" % c, align_bytes=64))
+            codes.append(keep.tile([P, CHUNK], U32, name="codes%d" % c, align_bytes=64))
+            scales.append(keep.tile([P, CHUNK], U8, name="scales%d" % c, align_bytes=64))
+            nc.sync.dma_start(out=raws[c][:], in_=view)
+
+        ident = keep.tile([P, P], F32, name="ident")
+        make_identity(nc, ident[:])
+        neg_half = keep.tile([P, 1], F32, name="neg_half")
+        nc.gpsimd.memset(neg_half[:], -0.5)
+        warm_in = keep.tile([P, 1], F32, name="warm_in")
+        warm_out = keep.tile([P, 1], F32, name="warm_out")
+        nc.vector.memset(warm_in[:], 0.0)
+        nc.scalar.activation(out=warm_out[:], in_=warm_in[:], func=ACT.Silu)
+        ln_f32 = keep.tile([P, PASSES, PACK], F32, name="ln_f32")
+        nc.gpsimd.tensor_copy(out=ln_f32[:], in_=ln_sb[:])
+
+        def regroup_part(copy, c, cols):
+            if c < 2 * PASSES:
+                ranks = slice(cols.start // P, cols.stop // P)
+                copy(
+                    out=groupeds[c][:, cols, :].rearrange("p (t m) j -> p t m j", m=P),
+                    in_=raws[c][:].rearrange("p j (m t) -> p t m j", t=PACK)[:, ranks],
+                )
+            else:
+                copy(
+                    out=groupeds[c][:, cols, :].rearrange("p (w i) j -> p w j i", i=RUN),
+                    in_=raws[c][:, :, cols].rearrange("p j (w i) -> p w j i", i=RUN),
+                )
+
+        def regroup(c):
+            regroup_part(nc.vector.tensor_copy, c, slice(0, VECTOR_COLS))
+            regroup_part(nc.scalar.copy, c, slice(VECTOR_COLS, CHUNK))
+
+        def quantise(c):
+            nc.vector.quantize_mx(
+                out=codes[c][:].bitcast(FP8X4),
+                scales=scales[c][:],
+                in_=groupeds[c][:].rearrange("p w j -> p (w j)"),
+            )
+
+        h_perm = keep.tile([P, PASSES, PACK, P], F32, name="h_perm")
+        squares = keep.tile([P, PASSES, K_PASS], BF16, name="squares")
+        mean_parts = keep.tile([P, PASSES], F32, name="mean_parts")
+        mean_sq = keep.tile([P, 1], F32, name="mean_sq")
+        rstd = keep.tile([P, 1], F32, name="rstd")
+        gained = keep.tile([P, PASSES, PACK, P], F32, name="gained")
+        n_grouped = keep.tile([P, PASSES, P, PACK], BF16, name="n_grouped", align_bytes=64)
+        n_codes = keep.tile([P, PASSES, P], U32, name="n_codes", align_bytes=64)
+        n_scales = keep.tile([P, PASSES, P], U8, name="n_scales", align_bytes=64)
+        hT = [psum.tile([P, PACK, P], F32, name="hT%d" % g, tag="bank%d" % g) for g in range(PASSES)]
+        rstd_rows = psum.tile([P, P], F32, name="rstd_rows", tag="bank2")
+
+        def add_square_transpose(g):
+            nc.vector.tensor_tensor(
+                out=h_perm[:, g],
+                in0=x_sb[:, g, :].rearrange("t (p j) -> t j p", j=PACK),
+                in1=res_sb[:, g, :].rearrange("t (p j) -> t j p", j=PACK),
+                op=ALU.add,
+            )
+            nc.scalar.activation(
+                out=squares[:, g, :],
+                in_=h_perm[:, g].rearrange("t j p -> t (j p)"),
+                func=ACT.Square,
+                scale=H**-0.5,
+                accum_out=mean_parts[:, g : g + 1],
+            )
+            for j in range(PACK):
+                nc.tensor.transpose(hT[g][:, j, :], h_perm[:, g, j, :], ident[:])
+
+        def reciprocal_std():
+            nc.gpsimd.tensor_scalar(
+                out=mean_sq[:],
+                in0=mean_parts[:, 0:1],
+                scalar1=mean_parts[:, 1:2],
+                scalar2=EPS,
+                op0=ALU.add,
+                op1=ALU.add,
+            )
+            nc.gpsimd.tensor_tensor(out=rstd[:], in0=mean_sq[:], in1=neg_half[:], op=ALU.pow)
+            nc.tensor.transpose(rstd_rows[:], rstd[:].to_broadcast([P, P]), ident[:])
+
+        def apply_gain(g):
+            for j in range(PACK):
+                nc.scalar.activation(
+                    out=gained[:, g, j, :],
+                    in_=hT[g][:, j, :],
+                    func=ACT.Copy,
+                    scale=ln_f32[:, g, j : j + 1],
+                )
+
+        def normalise(g):
+            nc.vector.tensor_tensor(
+                out=n_grouped[:, g],
+                in0=gained[:, g].rearrange("p j t -> p t j"),
+                in1=rstd_rows[:].unsqueeze(2).to_broadcast([P, P, PACK]),
+                op=ALU.mult,
+            )
+
+        def quantise_n():
+            nc.vector.quantize_mx(
+                out=n_codes[:].rearrange("p g t -> p (g t)").bitcast(FP8X4),
+                scales=n_scales[:].rearrange("p g t -> p (g t)"),
+                in_=n_grouped[:].rearrange("p g t j -> p (g t j)"),
+            )
+
+        rT = [
+            psum.tile([P, PACK, P], F32, name="rT%d" % m, tag="bank%d" % (3 + m))
+            for m in (GATE, UP)
+        ]
+        r_grouped = [
+            keep.tile([P, P, PACK], BF16, name="r_grouped%d" % m, align_bytes=64)
+            for m in (GATE, UP)
+        ]
+        r_codes = [
+            keep.tile([P, P], U32, name="r_codes%d" % m, align_bytes=64) for m in (GATE, UP)
+        ]
+        r_scales = [
+            keep.tile([P, P], U8, name="r_scales%d" % m, align_bytes=64) for m in (GATE, UP)
+        ]
+
+        def first_contraction(m):
+            for b in range(PACK):
+                for g in range(PASSES):
+                    c = m * PASSES + g
+                    nc.tensor.matmul_mx(
+                        out=rT[m][:, b, :],
+                        lhsT=codes[c][:, b * P : (b + 1) * P].bitcast(FP8X4),
+                        lhsT_scale=scales[c][:, b * P : (b + 1) * P],
+                        rhs=n_codes[:, g, :].bitcast(FP8X4),
+                        rhs_scale=n_scales[:, g, :],
+                        start=(g == 0),
+                        stop=(g == PASSES - 1),
+                    )
+
+        def round_r(m):
+            nc.scalar.copy(out=r_grouped[m][:], in_=rT[m][:].rearrange("p b t -> p t b"))
+
+        def quantise_r(m):
+            nc.vector.quantize_mx(
+                out=r_codes[m][:].bitcast(FP8X4),
+                scales=r_scales[m][:],
+                in_=r_grouped[m][:].rearrange("p t b -> p (t b)"),
+            )
+
+        products = [
+            [
+                psum.tile(
+                    [P, CHUNK],
+                    F32,
+                    name="product%d_%d" % (m, half),
+                    tag="bank%d" % ((5 + m * HALVES + half) % 8),
+                )
+                for half in range(HALVES)
+            ]
+            for m in (GATE, UP)
+        ]
+        gates = [keep.tile([P, CHUNK], F32, name="gate%d" % half) for half in range(HALVES)]
+        results = [keep.tile([P, CHUNK], F32, name="result%d" % half) for half in range(HALVES)]
+
+        def second_contraction(m, half):
+            c = 2 * PASSES + m * HALVES + half
+            nc.tensor.matmul_mx(
+                out=products[m][half][:],
+                lhsT=r_codes[m][:].bitcast(FP8X4),
+                lhsT_scale=r_scales[m][:],
+                rhs=codes[c][:].bitcast(FP8X4),
+                rhs_scale=scales[c][:],
+                start=True,
+                stop=True,
+            )
+
+        def silu_gate(half):
+            nc.scalar.activation(out=gates[half][:], in_=products[GATE][half][:], func=ACT.Silu)
+
+        def multiply_and_store(half):
+            nc.vector.tensor_tensor(
+                out=results[half][:], in0=gates[half][:], in1=products[UP][half][:], op=ALU.mult
+            )
+            nc.sync.dma_start(
+                out=out_rows[:, half * CHUNK : (half + 1) * CHUNK], in_=results[half][:]
+            )
+
+        add_square_transpose(0)
+        add_square_transpose(1)
+        reciprocal_std()
+        apply_gain(0)
+        apply_gain(1)
+        regroup_part(nc.vector.tensor_copy, 0, slice(0, CHUNK))
+        regroup(1)
+        quantise(0)
+        normalise(0)
+        normalise(1)
+        quantise_n()
+        quantise(1)
+        first_contraction(GATE)
+        regroup(2)
+        regroup(3)
+        quantise(2)
+        regroup(4)
+        quantise(3)
+        first_contraction(UP)
+        round_r(GATE)
+        regroup(5)
+        quantise_r(GATE)
+        quantise(4)
+        second_contraction(GATE, 0)
+        regroup(6)
+        quantise(5)
+        second_contraction(GATE, 1)
+        round_r(UP)
+        regroup(7)
+        quantise_r(UP)
+        quantise(6)
+        second_contraction(UP, 0)
+        silu_gate(0)
+        silu_gate(1)
+        quantise(7)
+        second_contraction(UP, 1)
+        multiply_and_store(0)
+        multiply_and_store(1)

@@ -46,23 +46,24 @@ def tile_neuronllamamlp_pa_s_kernel(
         ln_sb = keep.tile([P, PASSES, PACK], BF16, name="ln_sb")
         nc.scalar.dma_start(out=ln_sb[:], in_=ln_w.rearrange("(g p j) -> p g j", p=P, j=PACK))
 
-        chunk_views = []
+        raws, groupeds, codes, scales = [], [], [], []
         for w in (w_gate_v, w_up_v):
             for g in range(PASSES):
+                raw = keep.tile([P, PACK, CHUNK], BF16, name="raw%d" % len(raws))
                 rows = w[g * K_PASS : (g + 1) * K_PASS, :]
-                chunk_views.append(rows.rearrange("(p j) r -> p j r", j=PACK))
+                nc.sync.dma_start(out=raw[:], in_=rows.rearrange("(p j) r -> p j r", j=PACK))
+                raws.append(raw[:])
         for w in (w_gate_u, w_up_u):
+            raw = keep.tile([P, PACK, I], BF16, name="raw%d" % len(raws))
+            stripes = w.rearrange("(a b s) i -> b a s i", b=PACK, s=RUN)
+            for b in range(PACK):
+                nc.sync.dma_start(out=raw[:, b, :], in_=stripes[b])
             for half in range(HALVES):
-                cols = w[:, half * CHUNK : (half + 1) * CHUNK]
-                chunk_views.append(cols.rearrange("(p j) i -> p j i", j=PACK))
-
-        raws, groupeds, codes, scales = [], [], [], []
-        for c, view in enumerate(chunk_views):
-            raws.append(keep.tile([P, PACK, CHUNK], BF16, name="raw%d" % c))
+                raws.append(raw[:, :, half * CHUNK : (half + 1) * CHUNK])
+        for c in range(len(raws)):
             groupeds.append(keep.tile([P, CHUNK, PACK], BF16, name="grouped%d" % c, align_bytes=64))
             codes.append(keep.tile([P, CHUNK], U32, name="codes%d" % c, align_bytes=64))
             scales.append(keep.tile([P, CHUNK], U8, name="scales%d" % c, align_bytes=64))
-            nc.sync.dma_start(out=raws[c][:], in_=view)
 
         ident = keep.tile([P, P], F32, name="ident")
         make_identity(nc, ident[:])
@@ -77,10 +78,10 @@ def tile_neuronllamamlp_pa_s_kernel(
 
         def regroup_part(copy, c, cols):
             if c < 2 * PASSES:
-                ranks = slice(cols.start // P, cols.stop // P)
+                blocks = slice(cols.start // P, cols.stop // P)
                 copy(
-                    out=groupeds[c][:, cols, :].rearrange("p (t m) j -> p t m j", m=P),
-                    in_=raws[c][:].rearrange("p j (m t) -> p t m j", t=PACK)[:, ranks],
+                    out=groupeds[c][:, cols, :].rearrange("p (b a s) j -> p b a j s", a=P // RUN, s=RUN),
+                    in_=raws[c].rearrange("p j (a b s) -> p b a j s", b=PACK, s=RUN)[:, blocks],
                 )
             else:
                 copy(

@@ -100,34 +100,38 @@ def tile_neuronllamamlp_pa_s_kernel(
                 in_=groupeds[c][:].rearrange("p w j -> p (w j)"),
             )
 
-        h_perm = keep.tile([P, PASSES, PACK, P], F32, name="h_perm")
+        h = keep.tile([P, PASSES, K_PASS], F32, name="h")
         squares = keep.tile([P, PASSES, K_PASS], BF16, name="squares")
         mean_parts = keep.tile([P, PASSES], F32, name="mean_parts")
         mean_sq = keep.tile([P, 1], F32, name="mean_sq")
         rstd = keep.tile([P, 1], F32, name="rstd")
-        gained = keep.tile([P, PASSES, PACK, P], F32, name="gained")
+        n = keep.tile([P, PASSES, K_PASS], BF16, name="n")
         n_grouped = keep.tile([P, PASSES, P, PACK], BF16, name="n_grouped", align_bytes=64)
         n_codes = keep.tile([P, PASSES, P], U32, name="n_codes", align_bytes=64)
         n_scales = keep.tile([P, PASSES, P], U8, name="n_scales", align_bytes=64)
-        hT = [psum.tile([P, PACK, P], F32, name="hT%d" % g, tag="bank%d" % g) for g in range(PASSES)]
-        rstd_rows = psum.tile([P, P], F32, name="rstd_rows", tag="bank2")
+        ln_rows = [
+            psum.tile([P, PACK, P], F32, name="ln_rows%d" % g, tag="bank%d" % g)
+            for g in range(PASSES)
+        ]
+        nT = psum.tile([P, PASSES, PACK // 2, P], F32, name="nT", tag="bank2")
 
-        def add_square_transpose(g):
+        def spread_gain(g):
+            for j in range(PACK):
+                nc.tensor.transpose(
+                    ln_rows[g][:, j, :], ln_f32[:, g, j : j + 1].to_broadcast([P, P]), ident[:]
+                )
+
+        def add_and_square(g):
             nc.vector.tensor_tensor(
-                out=h_perm[:, g],
-                in0=x_sb[:, g, :].rearrange("t (p j) -> t j p", j=PACK),
-                in1=res_sb[:, g, :].rearrange("t (p j) -> t j p", j=PACK),
-                op=ALU.add,
+                out=h[:, g, :], in0=x_sb[:, g, :], in1=res_sb[:, g, :], op=ALU.add
             )
             nc.scalar.activation(
                 out=squares[:, g, :],
-                in_=h_perm[:, g].rearrange("t j p -> t (j p)"),
+                in_=h[:, g, :],
                 func=ACT.Square,
                 scale=H**-0.5,
                 accum_out=mean_parts[:, g : g + 1],
             )
-            for j in range(PACK):
-                nc.tensor.transpose(hT[g][:, j, :], h_perm[:, g, j, :], ident[:])
 
         def reciprocal_std():
             nc.gpsimd.tensor_scalar(
@@ -139,23 +143,27 @@ def tile_neuronllamamlp_pa_s_kernel(
                 op1=ALU.add,
             )
             nc.gpsimd.tensor_tensor(out=rstd[:], in0=mean_sq[:], in1=neg_half[:], op=ALU.pow)
-            nc.tensor.transpose(rstd_rows[:], rstd[:].to_broadcast([P, P]), ident[:])
-
-        def apply_gain(g):
-            for j in range(PACK):
-                nc.scalar.activation(
-                    out=gained[:, g, j, :],
-                    in_=hT[g][:, j, :],
-                    func=ACT.Copy,
-                    scale=ln_f32[:, g, j : j + 1],
-                )
 
         def normalise(g):
-            nc.vector.tensor_tensor(
-                out=n_grouped[:, g],
-                in0=gained[:, g].rearrange("p j t -> p t j"),
-                in1=rstd_rows[:].unsqueeze(2).to_broadcast([P, P, PACK]),
-                op=ALU.mult,
+            nc.vector.scalar_tensor_tensor(
+                out=n[:, g, :].rearrange("t (p j) -> t p j", j=PACK),
+                in0=h[:, g, :].rearrange("t (p j) -> t p j", j=PACK),
+                scalar=rstd[:],
+                in1=ln_rows[g][:].rearrange("t j p -> t p j"),
+                op0=ALU.mult,
+                op1=ALU.mult,
+            )
+            words = n[:, g, :].bitcast(F32)
+            for u in range(PACK // 2):
+                nc.tensor.transpose(nT[:, g, u, :], words[:, u :: PACK // 2], ident[:])
+
+        def group_n():
+            nc.scalar.copy(
+                out=n_grouped[:]
+                .rearrange("p g t j -> p (g t j)")
+                .bitcast(F32)
+                .rearrange("p (g t u) -> p g t u", g=PASSES, u=PACK // 2),
+                in_=nT[:].rearrange("p g u t -> p g t u"),
             )
 
         def quantise_n():
@@ -242,20 +250,22 @@ def tile_neuronllamamlp_pa_s_kernel(
                 out=out_rows[:, half * CHUNK : (half + 1) * CHUNK], in_=results[half][:]
             )
 
-        add_square_transpose(0)
-        add_square_transpose(1)
+        spread_gain(0)
+        spread_gain(1)
+        add_and_square(0)
+        add_and_square(1)
         reciprocal_std()
-        apply_gain(0)
-        apply_gain(1)
-        regroup_part(nc.vector.tensor_copy, 0, slice(0, CHUNK))
+        regroup_part(nc.vector.tensor_copy, 0, slice(0, 3 * P))
+        regroup_part(nc.scalar.copy, 0, slice(3 * P, CHUNK))
         regroup(1)
-        quantise(0)
         normalise(0)
         normalise(1)
-        quantise_n()
-        quantise(1)
-        first_contraction(GATE)
+        quantise(0)
         regroup(2)
+        group_n()
+        quantise(1)
+        quantise_n()
+        first_contraction(GATE)
         regroup(3)
         quantise(2)
         regroup(4)

@@ -20,7 +20,8 @@ HALVES = I // 512
 EPS = 1e-05
 CHUNK = 512
 RUN = 4
-VECTOR_COLS = 256
+WHOLE = slice(0, CHUNK)
+LEFT, RIGHT = slice(0, CHUNK // 2), slice(CHUNK // 2, CHUNK)
 GATE, UP = 0, 1
 
 FLOPS = 2 * P * (2 * H * R + 2 * R * I)
@@ -89,15 +90,18 @@ def tile_neuronllamamlp_pa_s_kernel(
                     in_=raws[c][:, :, cols].rearrange("p j (w i) -> p w j i", i=RUN),
                 )
 
-        def regroup(c):
-            regroup_part(nc.vector.tensor_copy, c, slice(0, VECTOR_COLS))
-            regroup_part(nc.scalar.copy, c, slice(VECTOR_COLS, CHUNK))
+        def regroup(c, cols=WHOLE, vector=CHUNK // 2):
+            middle = cols.start + vector
+            step = 2 * P if c < 2 * PASSES else CHUNK
+            for start in range(cols.start, middle, step):
+                regroup_part(nc.vector.tensor_copy, c, slice(start, min(start + step, middle)))
+            regroup_part(nc.scalar.copy, c, slice(middle, cols.stop))
 
-        def quantise(c):
+        def quantise(c, cols=WHOLE):
             nc.vector.quantize_mx(
-                out=codes[c][:].bitcast(FP8X4),
-                scales=scales[c][:],
-                in_=groupeds[c][:].rearrange("p w j -> p (w j)"),
+                out=codes[c][:, cols].bitcast(FP8X4),
+                scales=scales[c][:, cols],
+                in_=groupeds[c][:, cols, :].rearrange("p w j -> p (w j)"),
             )
 
         h = keep.tile([P, PASSES, K_PASS], F32, name="h")
@@ -227,14 +231,14 @@ def tile_neuronllamamlp_pa_s_kernel(
         gates = [keep.tile([P, CHUNK], F32, name="gate%d" % half) for half in range(HALVES)]
         results = [keep.tile([P, CHUNK], F32, name="result%d" % half) for half in range(HALVES)]
 
-        def second_contraction(m, half):
+        def second_contraction(m, half, cols=WHOLE):
             c = 2 * PASSES + m * HALVES + half
             nc.tensor.matmul_mx(
-                out=products[m][half][:],
+                out=products[m][half][:, cols],
                 lhsT=r_codes[m][:].bitcast(FP8X4),
                 lhsT_scale=r_scales[m][:],
-                rhs=codes[c][:].bitcast(FP8X4),
-                rhs_scale=scales[c][:],
+                rhs=codes[c][:, cols].bitcast(FP8X4),
+                rhs_scale=scales[c][:, cols],
                 start=True,
                 stop=True,
             )
@@ -242,12 +246,16 @@ def tile_neuronllamamlp_pa_s_kernel(
         def silu_gate(half):
             nc.scalar.activation(out=gates[half][:], in_=products[GATE][half][:], func=ACT.Silu)
 
-        def multiply_and_store(half):
+        def multiply_and_store(half, cols=WHOLE):
             nc.vector.tensor_tensor(
-                out=results[half][:], in0=gates[half][:], in1=products[UP][half][:], op=ALU.mult
+                out=results[half][:, cols],
+                in0=gates[half][:, cols],
+                in1=products[UP][half][:, cols],
+                op=ALU.mult,
             )
+            first = half * CHUNK
             nc.sync.dma_start(
-                out=out_rows[:, half * CHUNK : (half + 1) * CHUNK], in_=results[half][:]
+                out=out_rows[:, first + cols.start : first + cols.stop], in_=results[half][:, cols]
             )
 
         spread_gain(0)
@@ -255,8 +263,7 @@ def tile_neuronllamamlp_pa_s_kernel(
         add_and_square(0)
         add_and_square(1)
         reciprocal_std()
-        regroup_part(nc.vector.tensor_copy, 0, slice(0, 3 * P))
-        regroup_part(nc.scalar.copy, 0, slice(3 * P, CHUNK))
+        regroup(0, vector=3 * P)
         regroup(1)
         normalise(0)
         normalise(1)
@@ -264,29 +271,33 @@ def tile_neuronllamamlp_pa_s_kernel(
         regroup(2)
         group_n()
         quantise(1)
+        regroup(3)
         quantise_n()
         first_contraction(GATE)
-        regroup(3)
-        quantise(2)
         regroup(4)
+        quantise(2)
+        regroup(5)
         quantise(3)
         first_contraction(UP)
         round_r(GATE)
-        regroup(5)
+        regroup(6)
         quantise_r(GATE)
         quantise(4)
         second_contraction(GATE, 0)
-        regroup(6)
         quantise(5)
         second_contraction(GATE, 1)
         round_r(UP)
-        regroup(7)
         quantise_r(UP)
+        regroup(7, LEFT, vector=128)
+        regroup(7, RIGHT, vector=96)
         quantise(6)
         second_contraction(UP, 0)
         silu_gate(0)
         silu_gate(1)
-        quantise(7)
-        second_contraction(UP, 1)
+        quantise(7, LEFT)
+        second_contraction(UP, 1, LEFT)
+        quantise(7, RIGHT)
+        second_contraction(UP, 1, RIGHT)
         multiply_and_store(0)
-        multiply_and_store(1)
+        multiply_and_store(1, LEFT)
+        multiply_and_store(1, RIGHT)

@@ -68,6 +68,8 @@ def tile_neuronllamamlp_pa_s_kernel(
 
         ident = keep.tile([P, P], F32, name="ident")
         make_identity(nc, ident[:])
+        ident_bf16 = keep.tile([P, P], BF16, name="ident_bf16")
+        nc.gpsimd.tensor_copy(out=ident_bf16[:], in_=ident[:])
         neg_half = keep.tile([P, 1], F32, name="neg_half")
         nc.gpsimd.memset(neg_half[:], -0.5)
         warm_in = keep.tile([P, 1], F32, name="warm_in")
@@ -96,6 +98,22 @@ def tile_neuronllamamlp_pa_s_kernel(
             for start in range(cols.start, middle, step):
                 regroup_part(nc.vector.tensor_copy, c, slice(start, min(start + step, middle)))
             regroup_part(nc.scalar.copy, c, slice(middle, cols.stop))
+
+        def weave(c, cols, name, tag):
+            woven = psum.tile([P, cols.stop - cols.start, PACK], BF16, name=name, tag=tag)
+            for start in range(cols.start, cols.stop, P):
+                place = start - cols.start
+                nc.tensor.matmul(
+                    woven[:, place : place + P, :].rearrange("p w j -> p (w j)"),
+                    lhsT=ident_bf16[:],
+                    rhs=raws[c][:, :, start : start + P].rearrange("p j w -> p w j"),
+                    start=True,
+                    stop=True,
+                )
+            return woven
+
+        def copy_woven(c, cols, woven):
+            nc.scalar.copy(out=groupeds[c][:, cols, :], in_=woven[:])
 
         def quantise(c, cols=WHOLE):
             nc.vector.quantize_mx(
@@ -279,6 +297,8 @@ def tile_neuronllamamlp_pa_s_kernel(
         regroup(5)
         quantise(3)
         first_contraction(UP)
+        woven_left = weave(7, slice(P, 2 * P), "woven_left", "bank2")
+        woven_right = weave(7, RIGHT, "woven_right", "bank1")
         round_r(GATE)
         regroup(6)
         quantise_r(GATE)
@@ -288,8 +308,9 @@ def tile_neuronllamamlp_pa_s_kernel(
         second_contraction(GATE, 1)
         round_r(UP)
         quantise_r(UP)
-        regroup(7, LEFT, vector=128)
-        regroup(7, RIGHT, vector=96)
+        regroup_part(nc.vector.tensor_copy, 7, slice(0, P))
+        copy_woven(7, slice(P, 2 * P), woven_left)
+        copy_woven(7, RIGHT, woven_right)
         quantise(6)
         second_contraction(UP, 0)
         silu_gate(0)

@@ -18,10 +18,10 @@ I = 1024
 PASSES = H // K_PASS
 HALVES = I // 512
 EPS = 1e-05
-CHUNK = 512
+CHUNK = I // HALVES
 RUN = 4
-WHOLE = slice(0, CHUNK)
-LEFT, RIGHT = slice(0, CHUNK // 2), slice(CHUNK // 2, CHUNK)
+WHOLE = slice(0, I)
+LEFT, RIGHT = slice(0, CHUNK), slice(CHUNK, I)
 GATE, UP = 0, 1
 
 FLOPS = 2 * P * (2 * H * R + 2 * R * I)
@@ -45,26 +45,33 @@ def tile_neuronllamamlp_pa_s_kernel(
             nc.sync.dma_start(out=x_sb[:, g, :], in_=x_rows[:, cols])
             nc.sync.dma_start(out=res_sb[:, g, :], in_=res_rows[:, cols])
         ln_sb = keep.tile([P, PASSES, PACK], BF16, name="ln_sb")
-        nc.scalar.dma_start(out=ln_sb[:], in_=ln_w.rearrange("(g p j) -> p g j", p=P, j=PACK))
+        nc.sync.dma_start(out=ln_sb[:], in_=ln_w.rearrange("(g p j) -> p g j", p=P, j=PACK))
 
-        raws, groupeds, codes, scales = [], [], [], []
-        for w in (w_gate_v, w_up_v):
+        raw_v = [
+            keep.tile([P, PASSES, PACK, R], BF16, name="raw_v%d" % m) for m in (GATE, UP)
+        ]
+        raw_u = [keep.tile([P, PACK, I], BF16, name="raw_u%d" % m) for m in (GATE, UP)]
+        for m, w in ((GATE, w_gate_v), (UP, w_up_v)):
             for g in range(PASSES):
-                raw = keep.tile([P, PACK, CHUNK], BF16, name="raw%d" % len(raws))
                 rows = w[g * K_PASS : (g + 1) * K_PASS, :]
-                nc.sync.dma_start(out=raw[:], in_=rows.rearrange("(p j) r -> p j r", j=PACK))
-                raws.append(raw[:])
-        for w in (w_gate_u, w_up_u):
-            raw = keep.tile([P, PACK, I], BF16, name="raw%d" % len(raws))
+                nc.sync.dma_start(
+                    out=raw_v[m][:, g], in_=rows.rearrange("(p j) r -> p j r", j=PACK)
+                )
+        for m, w, widths in ((GATE, w_gate_u, (WHOLE,)), (UP, w_up_u, (LEFT, RIGHT))):
             stripes = w.rearrange("(a b s) i -> b a s i", b=PACK, s=RUN)
-            for b in range(PACK):
-                nc.sync.dma_start(out=raw[:, b, :], in_=stripes[b])
-            for half in range(HALVES):
-                raws.append(raw[:, :, half * CHUNK : (half + 1) * CHUNK])
-        for c in range(len(raws)):
-            groupeds.append(keep.tile([P, CHUNK, PACK], BF16, name="grouped%d" % c, align_bytes=64))
-            codes.append(keep.tile([P, CHUNK], U32, name="codes%d" % c, align_bytes=64))
-            scales.append(keep.tile([P, CHUNK], U8, name="scales%d" % c, align_bytes=64))
+            for cols in widths:
+                for b in range(PACK):
+                    nc.sync.dma_start(out=raw_u[m][:, b, cols], in_=stripes[b][:, :, cols])
+
+        factors = [
+            [
+                keep.tile([P, I, PACK], BF16, name="grouped_%s%d" % (f, m), align_bytes=64),
+                keep.tile([P, I], U32, name="codes_%s%d" % (f, m), align_bytes=64),
+                keep.tile([P, I], U8, name="scales_%s%d" % (f, m), align_bytes=64),
+            ]
+            for f, m in (("v", GATE), ("v", UP), ("u", GATE), ("u", UP))
+        ]
+        v_factors, u_factors = factors[:2], factors[2:]
 
         ident = keep.tile([P, P], F32, name="ident")
         make_identity(nc, ident[:])
@@ -79,47 +86,44 @@ def tile_neuronllamamlp_pa_s_kernel(
         ln_f32 = keep.tile([P, PASSES, PACK], F32, name="ln_f32")
         nc.gpsimd.tensor_copy(out=ln_f32[:], in_=ln_sb[:])
 
-        def regroup_part(copy, c, cols):
-            if c < 2 * PASSES:
-                blocks = slice(cols.start // P, cols.stop // P)
-                copy(
-                    out=groupeds[c][:, cols, :].rearrange("p (b a s) j -> p b a j s", a=P // RUN, s=RUN),
-                    in_=raws[c].rearrange("p j (a b s) -> p b a j s", b=PACK, s=RUN)[:, blocks],
-                )
-            else:
-                copy(
-                    out=groupeds[c][:, cols, :].rearrange("p (w i) j -> p w j i", i=RUN),
-                    in_=raws[c][:, :, cols].rearrange("p j (w i) -> p w j i", i=RUN),
-                )
+        def regroup_v(m, g):
+            grouped = v_factors[m][0]
+            src = raw_v[m][:, g].rearrange("p j (a b s) -> p b a j s", b=PACK, s=RUN)
+            dst = grouped[:, g * R : (g + 1) * R, :].rearrange(
+                "p (b a s) j -> p b a j s", b=PACK, s=RUN
+            )
+            nc.vector.tensor_copy(out=dst[:, : PACK // 2], in_=src[:, : PACK // 2])
+            nc.scalar.copy(out=dst[:, PACK // 2 :], in_=src[:, PACK // 2 :])
 
-        def regroup(c, cols=WHOLE, vector=CHUNK // 2):
-            middle = cols.start + vector
-            step = 2 * P if c < 2 * PASSES else CHUNK
-            for start in range(cols.start, middle, step):
-                regroup_part(nc.vector.tensor_copy, c, slice(start, min(start + step, middle)))
-            regroup_part(nc.scalar.copy, c, slice(middle, cols.stop))
+        def regroup_u(copy, m, start, stop):
+            grouped = u_factors[m][0]
+            copy(
+                out=grouped[:, start:stop, :].rearrange("p (w i) j -> p w j i", i=RUN),
+                in_=raw_u[m][:, :, start:stop].rearrange("p j (w i) -> p w j i", i=RUN),
+            )
 
-        def weave(c, cols, name, tag):
-            woven = psum.tile([P, cols.stop - cols.start, PACK], BF16, name=name, tag=tag)
-            for start in range(cols.start, cols.stop, P):
-                place = start - cols.start
+        def weave_u(m, start, stop, name, tag):
+            woven = psum.tile([P, stop - start, PACK], BF16, name=name, tag=tag)
+            for first in range(start, stop, P):
+                place = first - start
                 nc.tensor.matmul(
                     woven[:, place : place + P, :].rearrange("p w j -> p (w j)"),
                     lhsT=ident_bf16[:],
-                    rhs=raws[c][:, :, start : start + P].rearrange("p j w -> p w j"),
+                    rhs=raw_u[m][:, :, first : first + P].rearrange("p j w -> p w j"),
                     start=True,
                     stop=True,
                 )
             return woven
 
-        def copy_woven(c, cols, woven):
-            nc.scalar.copy(out=groupeds[c][:, cols, :], in_=woven[:])
+        def copy_woven(m, start, stop, woven):
+            nc.scalar.copy(out=u_factors[m][0][:, start:stop, :], in_=woven[:])
 
-        def quantise(c, cols=WHOLE):
+        def quantise(factor, cols):
+            grouped, codes, scales = factor
             nc.vector.quantize_mx(
-                out=codes[c][:, cols].bitcast(FP8X4),
-                scales=scales[c][:, cols],
-                in_=groupeds[c][:, cols, :].rearrange("p w j -> p (w j)"),
+                out=codes[:, cols].bitcast(FP8X4),
+                scales=scales[:, cols],
+                in_=grouped[:, cols, :].rearrange("p w j -> p (w j)"),
             )
 
         h = keep.tile([P, PASSES, K_PASS], F32, name="h")
@@ -211,13 +215,14 @@ def tile_neuronllamamlp_pa_s_kernel(
         ]
 
         def first_contraction(m):
+            codes, scales = v_factors[m][1:]
             for b in range(PACK):
                 for g in range(PASSES):
-                    c = m * PASSES + g
+                    cols = slice(g * R + b * P, g * R + (b + 1) * P)
                     nc.tensor.matmul_mx(
                         out=rT[m][:, b, :],
-                        lhsT=codes[c][:, b * P : (b + 1) * P].bitcast(FP8X4),
-                        lhsT_scale=scales[c][:, b * P : (b + 1) * P],
+                        lhsT=codes[:, cols].bitcast(FP8X4),
+                        lhsT_scale=scales[:, cols],
                         rhs=n_codes[:, g, :].bitcast(FP8X4),
                         rhs_scale=n_scales[:, g, :],
                         start=(g == 0),
@@ -249,14 +254,15 @@ def tile_neuronllamamlp_pa_s_kernel(
         gates = [keep.tile([P, CHUNK], F32, name="gate%d" % half) for half in range(HALVES)]
         results = [keep.tile([P, CHUNK], F32, name="result%d" % half) for half in range(HALVES)]
 
-        def second_contraction(m, half, cols=WHOLE):
-            c = 2 * PASSES + m * HALVES + half
+        def second_contraction(m, half):
+            codes, scales = u_factors[m][1:]
+            cols = slice(half * CHUNK, (half + 1) * CHUNK)
             nc.tensor.matmul_mx(
-                out=products[m][half][:, cols],
+                out=products[m][half][:],
                 lhsT=r_codes[m][:].bitcast(FP8X4),
                 lhsT_scale=r_scales[m][:],
-                rhs=codes[c][:, cols].bitcast(FP8X4),
-                rhs_scale=scales[c][:, cols],
+                rhs=codes[:, cols].bitcast(FP8X4),
+                rhs_scale=scales[:, cols],
                 start=True,
                 stop=True,
             )
@@ -264,16 +270,12 @@ def tile_neuronllamamlp_pa_s_kernel(
         def silu_gate(half):
             nc.scalar.activation(out=gates[half][:], in_=products[GATE][half][:], func=ACT.Silu)
 
-        def multiply_and_store(half, cols=WHOLE):
+        def multiply_and_store(half):
             nc.vector.tensor_tensor(
-                out=results[half][:, cols],
-                in0=gates[half][:, cols],
-                in1=products[UP][half][:, cols],
-                op=ALU.mult,
+                out=results[half][:], in0=gates[half][:], in1=products[UP][half][:], op=ALU.mult
             )
-            first = half * CHUNK
             nc.sync.dma_start(
-                out=out_rows[:, first + cols.start : first + cols.stop], in_=results[half][:, cols]
+                out=out_rows[:, half * CHUNK : (half + 1) * CHUNK], in_=results[half][:]
             )
 
         spread_gain(0)
@@ -281,44 +283,40 @@ def tile_neuronllamamlp_pa_s_kernel(
         add_and_square(0)
         add_and_square(1)
         reciprocal_std()
-        regroup(0, vector=3 * P)
-        regroup(1)
+        regroup_v(GATE, 0)
+        regroup_v(GATE, 1)
         normalise(0)
         normalise(1)
-        quantise(0)
-        regroup(2)
+        regroup_v(UP, 0)
         group_n()
-        quantise(1)
-        regroup(3)
+        quantise(v_factors[GATE], WHOLE)
+        regroup_v(UP, 1)
         quantise_n()
         first_contraction(GATE)
-        regroup(4)
-        quantise(2)
-        regroup(5)
-        quantise(3)
+        regroup_u(nc.vector.tensor_copy, GATE, 0, CHUNK)
+        regroup_u(nc.scalar.copy, GATE, CHUNK, CHUNK + 2 * P)
+        quantise(v_factors[UP], WHOLE)
+        woven_gate = weave_u(GATE, CHUNK + 2 * P, I, "woven_gate", "bank1")
         first_contraction(UP)
-        woven_left = weave(7, slice(P, 2 * P), "woven_left", "bank2")
-        woven_right = weave(7, RIGHT, "woven_right", "bank1")
         round_r(GATE)
-        regroup(6)
+        regroup_u(nc.vector.tensor_copy, UP, 0, CHUNK)
+        regroup_u(nc.scalar.copy, UP, CHUNK, CHUNK + 2 * P)
+        copy_woven(GATE, CHUNK + 2 * P, I, woven_gate)
         quantise_r(GATE)
-        quantise(4)
+        quantise(u_factors[GATE], LEFT)
         second_contraction(GATE, 0)
-        quantise(5)
+        woven_up = weave_u(UP, I - P, I, "woven_up", "bank2")
+        quantise(u_factors[GATE], RIGHT)
         second_contraction(GATE, 1)
         round_r(UP)
+        regroup_u(nc.scalar.copy, UP, CHUNK + 2 * P, I - P)
+        copy_woven(UP, I - P, I, woven_up)
         quantise_r(UP)
-        regroup_part(nc.vector.tensor_copy, 7, slice(0, P))
-        copy_woven(7, slice(P, 2 * P), woven_left)
-        copy_woven(7, RIGHT, woven_right)
-        quantise(6)
+        quantise(u_factors[UP], LEFT)
         second_contraction(UP, 0)
         silu_gate(0)
         silu_gate(1)
-        quantise(7, LEFT)
-        second_contraction(UP, 1, LEFT)
-        quantise(7, RIGHT)
-        second_contraction(UP, 1, RIGHT)
+        quantise(u_factors[UP], RIGHT)
+        second_contraction(UP, 1)
         multiply_and_store(0)
-        multiply_and_store(1, LEFT)
-        multiply_and_store(1, RIGHT)
+        multiply_and_store(1)

import concourse.mybir as mybir
from concourse.masks import make_identity

BF16 = mybir.dt.bfloat16
F32 = mybir.dt.float32
U32 = mybir.dt.uint32
U8 = mybir.dt.uint8
FP8X4 = mybir.dt.float8_e4m3fn_x4
ALU = mybir.AluOpType
ACT = mybir.ActivationFunctionType

P = 128
PACK = 4
K_PASS = P * PACK
H = 1024
R = 512
I = 1024
PASSES = H // K_PASS
HALVES = I // 512
EPS = 1e-05
CHUNK = I // HALVES
RUN = 4
WHOLE = slice(0, I)
LEFT, RIGHT = slice(0, CHUNK), slice(CHUNK, I)
GATE, UP = 0, 1

FLOPS = 2 * P * (2 * H * R + 2 * R * I)


def tile_neuronllamamlp_pa_s_kernel(
    tc, x, residual, ln_w, w_gate_v, w_gate_u, w_up_v, w_up_u, out
):
    nc = tc.nc
    x_rows = x.flatten_outer_dims()
    res_rows = residual.flatten_outer_dims()
    out_rows = out.flatten_outer_dims()

    with tc.tile_pool(name="keep", bufs=1) as keep, tc.psum_pool(
        name="psum", bufs=1
    ) as psum, tc.manual_schedule():
        x_sb = keep.tile([P, PASSES, K_PASS], BF16, name="x_sb")
        res_sb = keep.tile([P, PASSES, K_PASS], BF16, name="res_sb")
        for g in range(PASSES):
            cols = slice(g * K_PASS, (g + 1) * K_PASS)
            nc.sync.dma_start(out=x_sb[:, g, :], in_=x_rows[:, cols])
            nc.sync.dma_start(out=res_sb[:, g, :], in_=res_rows[:, cols])
        ln_sb = keep.tile([P, PASSES, PACK], BF16, name="ln_sb")
        nc.sync.dma_start(out=ln_sb[:], in_=ln_w.rearrange("(g p j) -> p g j", p=P, j=PACK))

        raw_v = [
            keep.tile([P, PASSES, PACK, R], BF16, name="raw_v%d" % m) for m in (GATE, UP)
        ]
        raw_u = [keep.tile([P, PACK, I], BF16, name="raw_u%d" % m) for m in (GATE, UP)]
        for m, w in ((GATE, w_gate_v), (UP, w_up_v)):
            for g in range(PASSES):
                rows = w[g * K_PASS : (g + 1) * K_PASS, :]
                nc.sync.dma_start(
                    out=raw_v[m][:, g], in_=rows.rearrange("(p j) r -> p j r", j=PACK)
                )
        for m, w, widths in ((GATE, w_gate_u, (WHOLE,)), (UP, w_up_u, (LEFT, RIGHT))):
            stripes = w.rearrange("(a b s) i -> b a s i", b=PACK, s=RUN)
            for cols in widths:
                for b in range(PACK):
                    nc.sync.dma_start(out=raw_u[m][:, b, cols], in_=stripes[b][:, :, cols])

        factors = [
            [
                keep.tile([P, I, PACK], BF16, name="grouped_%s%d" % (f, m), align_bytes=64),
                keep.tile([P, I], U32, name="codes_%s%d" % (f, m), align_bytes=64),
                keep.tile([P, I], U8, name="scales_%s%d" % (f, m), align_bytes=64),
            ]
            for f, m in (("v", GATE), ("v", UP), ("u", GATE), ("u", UP))
        ]
        v_factors, u_factors = factors[:2], factors[2:]

        ident = keep.tile([P, P], F32, name="ident")
        make_identity(nc, ident[:])
        ident_bf16 = keep.tile([P, P], BF16, name="ident_bf16")
        nc.gpsimd.tensor_copy(out=ident_bf16[:], in_=ident[:])
        neg_half = keep.tile([P, 1], F32, name="neg_half")
        nc.gpsimd.memset(neg_half[:], -0.5)
        warm_in = keep.tile([P, 1], F32, name="warm_in")
        warm_out = keep.tile([P, 1], F32, name="warm_out")
        nc.vector.memset(warm_in[:], 0.0)
        nc.scalar.activation(out=warm_out[:], in_=warm_in[:], func=ACT.Silu)
        ln_f32 = keep.tile([P, PASSES, PACK], F32, name="ln_f32")
        nc.gpsimd.tensor_copy(out=ln_f32[:], in_=ln_sb[:])

        def regroup_v(m, g):
            grouped = v_factors[m][0]
            src = raw_v[m][:, g].rearrange("p j (a b s) -> p b a j s", b=PACK, s=RUN)
            dst = grouped[:, g * R : (g + 1) * R, :].rearrange(
                "p (b a s) j -> p b a j s", b=PACK, s=RUN
            )
            nc.vector.tensor_copy(out=dst[:, : PACK // 2], in_=src[:, : PACK // 2])
            nc.scalar.copy(out=dst[:, PACK // 2 :], in_=src[:, PACK // 2 :])

        def regroup_u(copy, m, start, stop):
            grouped = u_factors[m][0]
            copy(
                out=grouped[:, start:stop, :].rearrange("p (w i) j -> p w j i", i=RUN),
                in_=raw_u[m][:, :, start:stop].rearrange("p j (w i) -> p w j i", i=RUN),
            )

        def weave_u(m, start, stop, name, tag):
            woven = psum.tile([P, stop - start, PACK], BF16, name=name, tag=tag)
            for first in range(start, stop, P):
                place = first - start
                nc.tensor.matmul(
                    woven[:, place : place + P, :].rearrange("p w j -> p (w j)"),
                    lhsT=ident_bf16[:],
                    rhs=raw_u[m][:, :, first : first + P].rearrange("p j w -> p w j"),
                    start=True,
                    stop=True,
                )
            return woven

        def copy_woven(m, start, stop, woven):
            nc.scalar.copy(out=u_factors[m][0][:, start:stop, :], in_=woven[:])

        def quantise(factor, cols):
            grouped, codes, scales = factor
            nc.vector.quantize_mx(
                out=codes[:, cols].bitcast(FP8X4),
                scales=scales[:, cols],
                in_=grouped[:, cols, :].rearrange("p w j -> p (w j)"),
            )

        h = keep.tile([P, PASSES, K_PASS], F32, name="h")
        squares = keep.tile([P, PASSES, K_PASS], BF16, name="squares")
        mean_parts = keep.tile([P, PASSES], F32, name="mean_parts")
        mean_sq = keep.tile([P, 1], F32, name="mean_sq")
        rstd = keep.tile([P, 1], F32, name="rstd")
        n = keep.tile([P, PASSES, K_PASS], BF16, name="n")
        n_grouped = keep.tile([P, PASSES, P, PACK], BF16, name="n_grouped", align_bytes=64)
        n_codes = keep.tile([P, PASSES, P], U32, name="n_codes", align_bytes=64)
        n_scales = keep.tile([P, PASSES, P], U8, name="n_scales", align_bytes=64)
        ln_rows = [
            psum.tile([P, PACK, P], F32, name="ln_rows%d" % g, tag="bank%d" % g)
            for g in range(PASSES)
        ]
        nT = psum.tile([P, PASSES, PACK // 2, P], F32, name="nT", tag="bank2")

        def spread_gain(g):
            for j in range(PACK):
                nc.tensor.transpose(
                    ln_rows[g][:, j, :], ln_f32[:, g, j : j + 1].to_broadcast([P, P]), ident[:]
                )

        def add_and_square(g):
            nc.vector.tensor_tensor(
                out=h[:, g, :], in0=x_sb[:, g, :], in1=res_sb[:, g, :], op=ALU.add
            )
            nc.scalar.activation(
                out=squares[:, g, :],
                in_=h[:, g, :],
                func=ACT.Square,
                scale=H**-0.5,
                accum_out=mean_parts[:, g : g + 1],
            )

        def reciprocal_std():
            nc.gpsimd.tensor_scalar(
                out=mean_sq[:],
                in0=mean_parts[:, 0:1],
                scalar1=mean_parts[:, 1:2],
                scalar2=EPS,
                op0=ALU.add,
                op1=ALU.add,
            )
            nc.gpsimd.tensor_tensor(out=rstd[:], in0=mean_sq[:], in1=neg_half[:], op=ALU.pow)

        def normalise(g):
            nc.vector.scalar_tensor_tensor(
                out=n[:, g, :].rearrange("t (p j) -> t p j", j=PACK),
                in0=h[:, g, :].rearrange("t (p j) -> t p j", j=PACK),
                scalar=rstd[:],
                in1=ln_rows[g][:].rearrange("t j p -> t p j"),
                op0=ALU.mult,
                op1=ALU.mult,
            )
            words = n[:, g, :].bitcast(F32)
            for u in range(PACK // 2):
                nc.tensor.transpose(nT[:, g, u, :], words[:, u :: PACK // 2], ident[:])

        def group_n():
            nc.scalar.copy(
                out=n_grouped[:]
                .rearrange("p g t j -> p (g t j)")
                .bitcast(F32)
                .rearrange("p (g t u) -> p g t u", g=PASSES, u=PACK // 2),
                in_=nT[:].rearrange("p g u t -> p g t u"),
            )

        def quantise_n():
            nc.vector.quantize_mx(
                out=n_codes[:].rearrange("p g t -> p (g t)").bitcast(FP8X4),
                scales=n_scales[:].rearrange("p g t -> p (g t)"),
                in_=n_grouped[:].rearrange("p g t j -> p (g t j)"),
            )

        rT = [
            psum.tile([P, PACK, P], F32, name="rT%d" % m, tag="bank%d" % (3 + m))
            for m in (GATE, UP)
        ]
        r_grouped = [
            keep.tile([P, P, PACK], BF16, name="r_grouped%d" % m, align_bytes=64)
            for m in (GATE, UP)
        ]
        r_codes = [
            keep.tile([P, P], U32, name="r_codes%d" % m, align_bytes=64) for m in (GATE, UP)
        ]
        r_scales = [
            keep.tile([P, P], U8, name="r_scales%d" % m, align_bytes=64) for m in (GATE, UP)
        ]

        def first_contraction(m):
            codes, scales = v_factors[m][1:]
            for b in range(PACK):
                for g in range(PASSES):
                    cols = slice(g * R + b * P, g * R + (b + 1) * P)
                    nc.tensor.matmul_mx(
                        out=rT[m][:, b, :],
                        lhsT=codes[:, cols].bitcast(FP8X4),
                        lhsT_scale=scales[:, cols],
                        rhs=n_codes[:, g, :].bitcast(FP8X4),
                        rhs_scale=n_scales[:, g, :],
                        start=(g == 0),
                        stop=(g == PASSES - 1),
                    )

        def round_r(m):
            nc.scalar.copy(out=r_grouped[m][:], in_=rT[m][:].rearrange("p b t -> p t b"))

        def quantise_r(m):
            nc.vector.quantize_mx(
                out=r_codes[m][:].bitcast(FP8X4),
                scales=r_scales[m][:],
                in_=r_grouped[m][:].rearrange("p t b -> p (t b)"),
            )

        products = [
            [
                psum.tile(
                    [P, CHUNK],
                    F32,
                    name="product%d_%d" % (m, half),
                    tag="bank%d" % ((5 + m * HALVES + half) % 8),
                )
                for half in range(HALVES)
            ]
            for m in (GATE, UP)
        ]
        gates = [keep.tile([P, CHUNK], F32, name="gate%d" % half) for half in range(HALVES)]
        results = [keep.tile([P, CHUNK], F32, name="result%d" % half) for half in range(HALVES)]

        def second_contraction(m, half):
            codes, scales = u_factors[m][1:]
            cols = slice(half * CHUNK, (half + 1) * CHUNK)
            nc.tensor.matmul_mx(
                out=products[m][half][:],
                lhsT=r_codes[m][:].bitcast(FP8X4),
                lhsT_scale=r_scales[m][:],
                rhs=codes[:, cols].bitcast(FP8X4),
                rhs_scale=scales[:, cols],
                start=True,
                stop=True,
            )

        def silu_gate(half):
            nc.scalar.activation(out=gates[half][:], in_=products[GATE][half][:], func=ACT.Silu)

        def multiply_and_store(half):
            nc.vector.tensor_tensor(
                out=results[half][:], in0=gates[half][:], in1=products[UP][half][:], op=ALU.mult
            )
            nc.sync.dma_start(
                out=out_rows[:, half * CHUNK : (half + 1) * CHUNK], in_=results[half][:]
            )

        spread_gain(0)
        spread_gain(1)
        add_and_square(0)
        add_and_square(1)
        reciprocal_std()
        regroup_v(GATE, 0)
        regroup_v(GATE, 1)
        normalise(0)
        normalise(1)
        regroup_v(UP, 0)
        group_n()
        quantise(v_factors[GATE], WHOLE)
        regroup_v(UP, 1)
        quantise_n()
        first_contraction(GATE)
        regroup_u(nc.vector.tensor_copy, GATE, 0, CHUNK)
        regroup_u(nc.scalar.copy, GATE, CHUNK, CHUNK + 2 * P)
        quantise(v_factors[UP], WHOLE)
        woven_gate = weave_u(GATE, CHUNK + 2 * P, I, "woven_gate", "bank1")
        first_contraction(UP)
        round_r(GATE)
        regroup_u(nc.vector.tensor_copy, UP, 0, CHUNK)
        regroup_u(nc.scalar.copy, UP, CHUNK, CHUNK + 2 * P)
        copy_woven(GATE, CHUNK + 2 * P, I, woven_gate)
        quantise_r(GATE)
        quantise(u_factors[GATE], LEFT)
        second_contraction(GATE, 0)
        woven_up = weave_u(UP, I - P, I, "woven_up", "bank2")
        quantise(u_factors[GATE], RIGHT)
        second_contraction(GATE, 1)
        round_r(UP)
        regroup_u(nc.scalar.copy, UP, CHUNK + 2 * P, I - P)
        copy_woven(UP, I - P, I, woven_up)
        quantise_r(UP)
        quantise(u_factors[UP], LEFT)
        second_contraction(UP, 0)
        silu_gate(0)
        silu_gate(1)
        quantise(u_factors[UP], RIGHT)
        second_contraction(UP, 1)
        multiply_and_store(0)
        multiply_and_store(1)
